import numpy as np
import ml_dtypes

BF16 = ml_dtypes.bfloat16


def bf(x):
    return np.asarray(x, np.float32).astype(BF16)


def f32(x):
    return np.asarray(x, np.float32)


def f64(x):
    return np.asarray(x).astype(np.float64)


def striped(idx):
    return np.tile(idx.reshape(-1, 16).T, (8, 1))


C, D, S, N, A, R, REQ = 1024, 1024, 2048, 1024, 8, 16, 16
K = A * R


def setup_inputs():
    base = f32(np.random.standard_normal((C, S)))
    x = bf(np.random.standard_normal((D, N)))
    w_q = bf(np.random.standard_normal((D, C)) / np.sqrt(D))
    a_w = bf(np.random.standard_normal((D, K)) / np.sqrt(D))
    b_w = bf(np.random.standard_normal((K, C)) / np.sqrt(R))
    scal = f32(np.repeat(0.5 + 0.5 * np.random.random_sample(A), R)[:, None])
    bins = np.random.permutation(np.tile(np.arange(A), REQ))[:REQ]
    sel = f32(np.repeat(np.arange(A), R)[:, None] == np.repeat(bins, N // REQ)[None, :])
    return {"base": base, "x": x, "w_q": w_q, "a_w": a_w, "b_w": b_w, "scal": scal, "sel": sel, "offs": striped(np.random.permutation(S)[:N])}


def reference(base, x, w_q, a_w, b_w, scal, sel, offs):
    idx = offs[:16].T.reshape(-1)
    proj = f64(w_q).T @ f64(x)
    h = (f64(a_w).T @ f64(x)) * f64(scal) * f64(sel)
    upd = f64(b_w).T @ h
    out = f64(base).copy()
    out[:, idx] = proj + upd
    return out

@@ -1,0 +1,73 @@
+import concourse.mybir as mybir
+
+BF16, F32, U16 = mybir.dt.bfloat16, mybir.dt.float32, mybir.dt.uint16
+MULT, ADD = mybir.AluOpType.mult, mybir.AluOpType.add
+
+P = 128
+C, D, S, N, K = 1024, 1024, 2048, 1024, 128
+C_BLOCKS, D_BLOCKS = C // P, D // P
+BANK = 512
+TOKEN_PIECES = [slice(t, t + BANK) for t in range(0, N, BANK)]
+
+FLOPS = 2 * N * (D * C + D * K + K * C)
+
+
+def tile_qkvparallellinearwithlora_b_kernel(tc, base, x, w_q, a_w, b_w, scal, sel, offs, out):
+    nc = tc.nc
+    with (
+        tc.tile_pool(name="held", bufs=1) as held,
+        tc.tile_pool(name="windows", bufs=2) as windows,
+        tc.tile_pool(name="staged", bufs=2) as staged,
+        tc.psum_pool(name="proj_banks", bufs=4) as proj_banks,
+        tc.psum_pool(name="lora_banks", bufs=4) as lora_banks,
+    ):
+        offsets = held.tile([P, N // 16], U16, name="offsets")
+        nc.sync.dma_start(offsets[:], offs)
+
+        a_sb = held.tile([P, D_BLOCKS, K], BF16, name="a_sb")
+        nc.sync.dma_start(a_sb[:], a_w.rearrange("(db p) k -> p db k", p=P))
+        x_sb, w_sb = [], []
+        for db in range(D_BLOCKS):
+            d_rows = slice(db * P, (db + 1) * P)
+            x_blk = held.tile([P, N], BF16, name=f"x{db}")
+            nc.sync.dma_start(x_blk[:], x[d_rows, :])
+            x_sb.append(x_blk)
+            w_blk = held.tile([P, C], BF16, name=f"w{db}")
+            nc.sync.dma_start(w_blk[:], w_q[d_rows, :])
+            w_sb.append(w_blk)
+        scal_sb = held.tile([P, 1], F32, name="scal_sb")
+        nc.sync.dma_start(scal_sb[:], scal)
+        sel_sb = held.tile([P, N], F32, name="sel_sb")
+        nc.sync.dma_start(sel_sb[:], sel)
+        b_sb = held.tile([P, C], BF16, name="b_sb")
+        nc.sync.dma_start(b_sb[:], b_w)
+
+        h_sb = held.tile([P, N], BF16, name="h_sb")
+        for tokens in TOKEN_PIECES:
+            h_ps = lora_banks.tile([P, BANK], F32, tag="lora")
+            for db in range(D_BLOCKS):
+                nc.tensor.matmul(
+                    h_ps[:], a_sb[:, db, :], x_sb[db][:, tokens], start=db == 0, stop=db == D_BLOCKS - 1
+                )
+            nc.vector.scalar_tensor_tensor(h_sb[:, tokens], h_ps[:], scal_sb[:, 0:1], sel_sb[:, tokens], MULT, MULT)
+
+        for cb in range(C_BLOCKS):
+            c_span = slice(cb * P, (cb + 1) * P)
+            window = windows.tile([P, S], F32, name="window")
+            nc.sync.dma_start(window[:], base[c_span, :])
+
+            proj_sb = staged.tile([P, N], F32, name="proj_sb")
+            upd_sb = staged.tile([P, N], F32, name="upd_sb")
+            for tokens in TOKEN_PIECES:
+                proj_ps = proj_banks.tile([P, BANK], F32, name="proj_ps")
+                for db in range(D_BLOCKS):
+                    nc.tensor.matmul(
+                        proj_ps[:], w_sb[db][:, c_span], x_sb[db][:, tokens], start=db == 0, stop=db == D_BLOCKS - 1
+                    )
+                nc.scalar.copy(proj_sb[:, tokens], proj_ps[:])
+                upd_ps = lora_banks.tile([P, BANK], F32, tag="lora")
+                nc.tensor.matmul(upd_ps[:], b_sb[:, c_span], h_sb[:, tokens], start=True, stop=True)
+                nc.scalar.copy(upd_sb[:, tokens], upd_ps[:])
+
+            nc.vector.tensor_tensor(window[:].indirect(offsets[:]), proj_sb[:], upd_sb[:], ADD)
+            nc.sync.dma_start(out[c_span, :], window[:])

@@ -16,8 +16,7 @@ def tile_qkvparallellinearwithlora_b_kernel(tc, base, x, w_q, a_w, b_w, scal, se
     nc = tc.nc
     with (
         tc.tile_pool(name="held", bufs=1) as held,
-        tc.tile_pool(name="windows", bufs=2) as windows,
-        tc.tile_pool(name="staged", bufs=2) as staged,
+        tc.tile_pool(name="staged", bufs=C_BLOCKS) as staged,
         tc.psum_pool(name="proj_banks", bufs=4) as proj_banks,
         tc.psum_pool(name="lora_banks", bufs=4) as lora_banks,
     ):
@@ -26,21 +25,28 @@ def tile_qkvparallellinearwithlora_b_kernel(tc, base, x, w_q, a_w, b_w, scal, se
 
         a_sb = held.tile([P, D_BLOCKS, K], BF16, name="a_sb")
         nc.sync.dma_start(a_sb[:], a_w.rearrange("(db p) k -> p db k", p=P))
-        x_sb, w_sb = [], []
+        x_sb = []
         for db in range(D_BLOCKS):
-            d_rows = slice(db * P, (db + 1) * P)
             x_blk = held.tile([P, N], BF16, name=f"x{db}")
-            nc.sync.dma_start(x_blk[:], x[d_rows, :])
+            nc.sync.dma_start(x_blk[:], x[db * P : (db + 1) * P, :])
             x_sb.append(x_blk)
-            w_blk = held.tile([P, C], BF16, name=f"w{db}")
-            nc.sync.dma_start(w_blk[:], w_q[d_rows, :])
-            w_sb.append(w_blk)
-        scal_sb = held.tile([P, 1], F32, name="scal_sb")
-        nc.sync.dma_start(scal_sb[:], scal)
-        sel_sb = held.tile([P, N], F32, name="sel_sb")
-        nc.sync.dma_start(sel_sb[:], sel)
-        b_sb = held.tile([P, C], BF16, name="b_sb")
-        nc.sync.dma_start(b_sb[:], b_w)
+
+        w_sb, windows = [], []
+        for cb in range(C_BLOCKS):
+            if cb % 2 == 0:
+                w_strip = held.tile([P, D_BLOCKS, 2 * P], BF16, name=f"w{cb // 2}")
+                nc.sync.dma_start(w_strip[:], w_q[:, cb * P : (cb + 2) * P].rearrange("(db p) c -> p db c", p=P))
+                w_sb.append(w_strip)
+            if cb == 0:
+                scal_sb = held.tile([P, 1], F32, name="scal_sb")
+                nc.sync.dma_start(scal_sb[:], scal)
+                sel_sb = held.tile([P, N], F32, name="sel_sb")
+                nc.sync.dma_start(sel_sb[:], sel)
+                b_sb = held.tile([P, C], BF16, name="b_sb")
+                nc.sync.dma_start(b_sb[:], b_w)
+            window = held.tile([P, S], F32, name=f"window{cb}")
+            nc.sync.dma_start(window[:], base[cb * P : (cb + 1) * P, :])
+            windows.append(window)
 
         h_sb = held.tile([P, N], BF16, name="h_sb")
         for tokens in TOKEN_PIECES:
@@ -53,21 +59,20 @@ def tile_qkvparallellinearwithlora_b_kernel(tc, base, x, w_q, a_w, b_w, scal, se
 
         for cb in range(C_BLOCKS):
             c_span = slice(cb * P, (cb + 1) * P)
-            window = windows.tile([P, S], F32, name="window")
-            nc.sync.dma_start(window[:], base[c_span, :])
-
+            w_strip, in_strip = w_sb[cb // 2], slice((cb % 2) * P, (cb % 2 + 1) * P)
             proj_sb = staged.tile([P, N], F32, name="proj_sb")
             upd_sb = staged.tile([P, N], F32, name="upd_sb")
+            for tokens in TOKEN_PIECES:
+                upd_ps = lora_banks.tile([P, BANK], F32, tag="lora")
+                nc.tensor.matmul(upd_ps[:], b_sb[:, c_span], h_sb[:, tokens], start=True, stop=True)
+                nc.scalar.copy(upd_sb[:, tokens], upd_ps[:])
             for tokens in TOKEN_PIECES:
                 proj_ps = proj_banks.tile([P, BANK], F32, name="proj_ps")
                 for db in range(D_BLOCKS):
                     nc.tensor.matmul(
-                        proj_ps[:], w_sb[db][:, c_span], x_sb[db][:, tokens], start=db == 0, stop=db == D_BLOCKS - 1
+                        proj_ps[:], w_strip[:, db, in_strip], x_sb[db][:, tokens], start=db == 0, stop=db == D_BLOCKS - 1
                     )
                 nc.scalar.copy(proj_sb[:, tokens], proj_ps[:])
-                upd_ps = lora_banks.tile([P, BANK], F32, tag="lora")
-                nc.tensor.matmul(upd_ps[:], b_sb[:, c_span], h_sb[:, tokens], start=True, stop=True)
-                nc.scalar.copy(upd_sb[:, tokens], upd_ps[:])
 
-            nc.vector.tensor_tensor(window[:].indirect(offsets[:]), proj_sb[:], upd_sb[:], ADD)
-            nc.sync.dma_start(out[c_span, :], window[:])
+            nc.vector.tensor_tensor(windows[cb][:].indirect(offsets[:]), proj_sb[:], upd_sb[:], ADD)
+            nc.sync.dma_start(out[c_span, :], windows[cb][:])

@@ -8,6 +8,7 @@ C, D, S, N, K = 1024, 1024, 2048, 1024, 128
 C_BLOCKS, D_BLOCKS = C // P, D // P
 BANK = 512
 TOKEN_PIECES = [slice(t, t + BANK) for t in range(0, N, BANK)]
+WARM_UP_MATMULS = 6
 
 FLOPS = 2 * N * (D * C + D * K + K * C)
 
@@ -22,6 +23,12 @@ def tile_qkvparallellinearwithlora_b_kernel(tc, base, x, w_q, a_w, b_w, scal, se
     ):
         offsets = held.tile([P, N // 16], U16, name="offsets")
         nc.sync.dma_start(offsets[:], offs)
+
+        zeros = held.tile([P, BANK], BF16, name="zeros")
+        nc.gpsimd.memset(zeros[:], 0.0)
+        unread_ps = lora_banks.tile([P, BANK], F32, tag="lora")
+        for i in range(WARM_UP_MATMULS):
+            nc.tensor.matmul(unread_ps[:], zeros[:, 0:P], zeros[:], start=True, stop=True)
 
         a_sb = held.tile([P, D_BLOCKS, K], BF16, name="a_sb")
         nc.sync.dma_start(a_sb[:], a_w.rearrange("(db p) k -> p db k", p=P))

@@ -8,7 +8,8 @@ C, D, S, N, K = 1024, 1024, 2048, 1024, 128
 C_BLOCKS, D_BLOCKS = C // P, D // P
 BANK = 512
 TOKEN_PIECES = [slice(t, t + BANK) for t in range(0, N, BANK)]
-WARM_UP_MATMULS = 6
+HALF = D_BLOCKS // 2
+WARM_UP_MATMULS = 3
 
 FLOPS = 2 * N * (D * C + D * K + K * C)
 
@@ -21,63 +22,97 @@ def tile_qkvparallellinearwithlora_b_kernel(tc, base, x, w_q, a_w, b_w, scal, se
         tc.psum_pool(name="proj_banks", bufs=4) as proj_banks,
         tc.psum_pool(name="lora_banks", bufs=4) as lora_banks,
     ):
-        offsets = held.tile([P, N // 16], U16, name="offsets")
-        nc.sync.dma_start(offsets[:], offs)
-
         zeros = held.tile([P, BANK], BF16, name="zeros")
         nc.gpsimd.memset(zeros[:], 0.0)
         unread_ps = lora_banks.tile([P, BANK], F32, tag="lora")
         for i in range(WARM_UP_MATMULS):
             nc.tensor.matmul(unread_ps[:], zeros[:, 0:P], zeros[:], start=True, stop=True)
 
-        a_sb = held.tile([P, D_BLOCKS, K], BF16, name="a_sb")
-        nc.sync.dma_start(a_sb[:], a_w.rearrange("(db p) k -> p db k", p=P))
-        x_sb = []
-        for db in range(D_BLOCKS):
-            x_blk = held.tile([P, N], BF16, name=f"x{db}")
-            nc.sync.dma_start(x_blk[:], x[db * P : (db + 1) * P, :])
-            x_sb.append(x_blk)
+        x_blocks = x.rearrange("(p db) n -> p db n", db=D_BLOCKS)
+        w_blocks = w_q.rearrange("(p db) c -> p db c", db=D_BLOCKS)
+        a_blocks = a_w.rearrange("(p db) k -> p db k", db=D_BLOCKS)
+        x_sb = {}
+        w_sb = {}
+        a_sb = {}
+        pieces = list(enumerate(TOKEN_PIECES))
 
-        w_sb, windows = [], []
+        def load_x(db, split):
+            if split:
+                for t, tokens in pieces:
+                    x_piece = held.tile([P, BANK], BF16, name=f"x{db}_{t}")
+                    nc.sync.dma_start(x_piece[:], x_blocks[:, db, tokens])
+                    x_sb[db, t] = x_piece[:]
+            else:
+                x_blk = held.tile([P, N], BF16, name=f"x{db}")
+                nc.sync.dma_start(x_blk[:], x_blocks[:, db, :])
+                for t, tokens in pieces:
+                    x_sb[db, t] = x_blk[:, tokens]
+
+        def load_w(cb, half):
+            w_sb[cb, half] = held.tile([P, HALF, P], BF16, name=f"w{cb}_{half}")
+            nc.sync.dma_start(
+                w_sb[cb, half][:], w_blocks[:, half * HALF : (half + 1) * HALF, cb * P : (cb + 1) * P]
+            )
+
+        def load_a(half):
+            a_sb[half] = held.tile([P, HALF, K], BF16, name=f"a{half}")
+            nc.sync.dma_start(a_sb[half][:], a_blocks[:, half * HALF : (half + 1) * HALF, :])
+
+        for half in range(2):
+            load_a(half)
+            for db in range(half * HALF, (half + 1) * HALF):
+                load_x(db, split=db == 0)
+                if db == half * HALF:
+                    load_w(0, half)
+
+        sel_sb = held.tile([P, N], F32, name="sel_sb")
+        nc.sync.dma_start(sel_sb[:], sel)
+        scal_sb = held.tile([P, 1], F32, name="scal_sb")
+        nc.sync.dma_start(scal_sb[:], scal)
+        b_sb = held.tile([P, C], BF16, name="b_sb")
+        nc.sync.dma_start(b_sb[:], b_w)
+
+        offsets = held.tile([P, N // 16], U16, name="offsets")
+        nc.sync.dma_start(offsets[:], offs)
+
+        windows = []
         for cb in range(C_BLOCKS):
-            if cb % 2 == 0:
-                w_strip = held.tile([P, D_BLOCKS, 2 * P], BF16, name=f"w{cb // 2}")
-                nc.sync.dma_start(w_strip[:], w_q[:, cb * P : (cb + 2) * P].rearrange("(db p) c -> p db c", p=P))
-                w_sb.append(w_strip)
-            if cb == 0:
-                scal_sb = held.tile([P, 1], F32, name="scal_sb")
-                nc.sync.dma_start(scal_sb[:], scal)
-                sel_sb = held.tile([P, N], F32, name="sel_sb")
-                nc.sync.dma_start(sel_sb[:], sel)
-                b_sb = held.tile([P, C], BF16, name="b_sb")
-                nc.sync.dma_start(b_sb[:], b_w)
             window = held.tile([P, S], F32, name=f"window{cb}")
             nc.sync.dma_start(window[:], base[cb * P : (cb + 1) * P, :])
             windows.append(window)
+            if cb + 1 < C_BLOCKS:
+                load_w(cb + 1, 0)
+                load_w(cb + 1, 1)
 
         h_sb = held.tile([P, N], BF16, name="h_sb")
-        for tokens in TOKEN_PIECES:
+        for t, tokens in pieces:
             h_ps = lora_banks.tile([P, BANK], F32, tag="lora")
             for db in range(D_BLOCKS):
                 nc.tensor.matmul(
-                    h_ps[:], a_sb[:, db, :], x_sb[db][:, tokens], start=db == 0, stop=db == D_BLOCKS - 1
+                    h_ps[:], a_sb[db // HALF][:, db % HALF, :], x_sb[db, t], start=db == 0, stop=db == D_BLOCKS - 1
                 )
             nc.vector.scalar_tensor_tensor(h_sb[:, tokens], h_ps[:], scal_sb[:, 0:1], sel_sb[:, tokens], MULT, MULT)
 
         for cb in range(C_BLOCKS):
             c_span = slice(cb * P, (cb + 1) * P)
-            w_strip, in_strip = w_sb[cb // 2], slice((cb % 2) * P, (cb % 2 + 1) * P)
             proj_sb = staged.tile([P, N], F32, name="proj_sb")
             upd_sb = staged.tile([P, N], F32, name="upd_sb")
-            for tokens in TOKEN_PIECES:
+            for t, tokens in pieces:
                 upd_ps = lora_banks.tile([P, BANK], F32, tag="lora")
                 nc.tensor.matmul(upd_ps[:], b_sb[:, c_span], h_sb[:, tokens], start=True, stop=True)
-                nc.scalar.copy(upd_sb[:, tokens], upd_ps[:])
-            for tokens in TOKEN_PIECES:
+                if cb == 0:
+                    nc.vector.tensor_copy(upd_sb[:, tokens], upd_ps[:])
+                else:
+                    nc.scalar.copy(upd_sb[:, tokens], upd_ps[:])
+            for t, tokens in pieces:
                 proj_ps = proj_banks.tile([P, BANK], F32, name="proj_ps")
                 for db in range(D_BLOCKS):
                     nc.tensor.matmul(
-                        proj_ps[:], w_strip[:, db, in_strip], x_sb[db][:, tokens], start=db == 0, stop=db == D_BLOCKS - 1
+                        proj_ps[:],
+                        w_sb[cb, db // HALF][:, db % HALF, :],
+                        x_sb[db, t],
+                        start=db == 0,
+                        stop=db == D_BLOCKS - 1,
                     )
                 nc.scalar.copy(proj_sb[:, tokens], proj_ps[:])
 

@@ -9,6 +9,7 @@ C_BLOCKS, D_BLOCKS = C // P, D // P
 BANK = 512
 TOKEN_PIECES = [slice(t, t + BANK) for t in range(0, N, BANK)]
 HALF = D_BLOCKS // 2
+SUMS_IN_A_BLOCK = 4
 WARM_UP_MATMULS = 3
 
 FLOPS = 2 * N * (D * C + D * K + K * C)
@@ -19,12 +20,11 @@ def tile_qkvparallellinearwithlora_b_kernel(tc, base, x, w_q, a_w, b_w, scal, se
     with (
         tc.tile_pool(name="held", bufs=1) as held,
         tc.tile_pool(name="staged", bufs=C_BLOCKS) as staged,
-        tc.psum_pool(name="proj_banks", bufs=4) as proj_banks,
-        tc.psum_pool(name="lora_banks", bufs=4) as lora_banks,
+        tc.psum_pool(name="banks", bufs=SUMS_IN_A_BLOCK) as banks,
     ):
         zeros = held.tile([P, BANK], BF16, name="zeros")
         nc.gpsimd.memset(zeros[:], 0.0)
-        unread_ps = lora_banks.tile([P, BANK], F32, tag="lora")
+        unread_ps = banks.tile([P, BANK], F32, tag="sum")
         for i in range(WARM_UP_MATMULS):
             nc.tensor.matmul(unread_ps[:], zeros[:, 0:P], zeros[:], start=True, stop=True)
 
@@ -86,26 +86,22 @@ def tile_qkvparallellinearwithlora_b_kernel(tc, base, x, w_q, a_w, b_w, scal, se
 
         h_sb = held.tile([P, N], BF16, name="h_sb")
         for t, tokens in pieces:
-            h_ps = lora_banks.tile([P, BANK], F32, tag="lora")
+            h_ps = banks.tile([P, BANK], F32, tag="sum")
             for db in range(D_BLOCKS):
                 nc.tensor.matmul(
                     h_ps[:], a_sb[db // HALF][:, db % HALF, :], x_sb[db, t], start=db == 0, stop=db == D_BLOCKS - 1
                 )
             nc.vector.scalar_tensor_tensor(h_sb[:, tokens], h_ps[:], scal_sb[:, 0:1], sel_sb[:, tokens], MULT, MULT)
 
+        def copy_out(cb, t):
+            return nc.vector.tensor_copy if cb == 0 and t == len(pieces) - 1 else nc.scalar.copy
+
         for cb in range(C_BLOCKS):
             c_span = slice(cb * P, (cb + 1) * P)
             proj_sb = staged.tile([P, N], F32, name="proj_sb")
             upd_sb = staged.tile([P, N], F32, name="upd_sb")
             for t, tokens in pieces:
-                upd_ps = lora_banks.tile([P, BANK], F32, tag="lora")
-                nc.tensor.matmul(upd_ps[:], b_sb[:, c_span], h_sb[:, tokens], start=True, stop=True)
-                if cb == 0:
-                    nc.vector.tensor_copy(upd_sb[:, tokens], upd_ps[:])
-                else:
-                    nc.scalar.copy(upd_sb[:, tokens], upd_ps[:])
-            for t, tokens in pieces:
-                proj_ps = proj_banks.tile([P, BANK], F32, name="proj_ps")
+                proj_ps = banks.tile([P, BANK], F32, tag="sum")
                 for db in range(D_BLOCKS):
                     nc.tensor.matmul(
                         proj_ps[:],
@@ -114,7 +110,11 @@ def tile_qkvparallellinearwithlora_b_kernel(tc, base, x, w_q, a_w, b_w, scal, se
                         start=db == 0,
                         stop=db == D_BLOCKS - 1,
                     )
-                nc.scalar.copy(proj_sb[:, tokens], proj_ps[:])
+                copy_out(cb, t)(proj_sb[:, tokens], proj_ps[:])
+            for t, tokens in pieces:
+                upd_ps = banks.tile([P, BANK], F32, tag="sum")
+                nc.tensor.matmul(upd_ps[:], b_sb[:, c_span], h_sb[:, tokens], start=True, stop=True)
+                copy_out(cb, t)(upd_sb[:, tokens], upd_ps[:])
 
             nc.vector.tensor_tensor(windows[cb][:].indirect(offsets[:]), proj_sb[:], upd_sb[:], ADD)
             nc.sync.dma_start(out[c_span, :], windows[cb][:])

@@ -8,8 +8,10 @@ C, D, S, N, K = 1024, 1024, 2048, 1024, 128
 C_BLOCKS, D_BLOCKS = C // P, D // P
 BANK = 512
 TOKEN_PIECES = [slice(t, t + BANK) for t in range(0, N, BANK)]
+LAST = BANK // 4
+PROJ_PIECES = [slice(0, BANK), slice(BANK, N - LAST), slice(N - LAST, N)]
 HALF = D_BLOCKS // 2
-SUMS_IN_A_BLOCK = 4
+SUM_BANKS, LATE_BANKS = 4, 1
 WARM_UP_MATMULS = 3
 
 FLOPS = 2 * N * (D * C + D * K + K * C)
@@ -20,7 +22,8 @@ def tile_qkvparallellinearwithlora_b_kernel(tc, base, x, w_q, a_w, b_w, scal, se
     with (
         tc.tile_pool(name="held", bufs=1) as held,
         tc.tile_pool(name="staged", bufs=C_BLOCKS) as staged,
-        tc.psum_pool(name="banks", bufs=SUMS_IN_A_BLOCK) as banks,
+        tc.psum_pool(name="banks", bufs=SUM_BANKS) as banks,
+        tc.psum_pool(name="late_bank", bufs=LATE_BANKS) as late_bank,
     ):
         zeros = held.tile([P, BANK], BF16, name="zeros")
         nc.gpsimd.memset(zeros[:], 0.0)
@@ -93,28 +96,36 @@ def tile_qkvparallellinearwithlora_b_kernel(tc, base, x, w_q, a_w, b_w, scal, se
                 )
             nc.vector.scalar_tensor_tensor(h_sb[:, tokens], h_ps[:], scal_sb[:, 0:1], sel_sb[:, tokens], MULT, MULT)
 
-        def copy_out(cb, t):
-            return nc.vector.tensor_copy if cb == 0 and t == len(pieces) - 1 else nc.scalar.copy
+        def update(cb, t):
+            ps = banks.tile([P, BANK], F32, name="upd_ps", tag="sum")
+            nc.tensor.matmul(ps[:], b_sb[:, cb * P : (cb + 1) * P], h_sb[:, TOKEN_PIECES[t]], start=True, stop=True)
+            return ps[:]
+
+        def project(cb, tokens, pool, tag):
+            ps = pool.tile([P, BANK], F32, name="proj_ps", tag=tag)
+            width = tokens.stop - tokens.start
+            t = tokens.start // BANK
+            columns = slice(tokens.start - t * BANK, tokens.stop - t * BANK)
+            for db in range(D_BLOCKS):
+                nc.tensor.matmul(
+                    ps[:, 0:width],
+                    w_sb[cb, db // HALF][:, db % HALF, :],
+                    x_sb[db, t][:, columns],
+                    start=db == 0,
+                    stop=db == D_BLOCKS - 1,
+                )
+            return ps[:, 0:width]
 
         for cb in range(C_BLOCKS):
             c_span = slice(cb * P, (cb + 1) * P)
             proj_sb = staged.tile([P, N], F32, name="proj_sb")
             upd_sb = staged.tile([P, N], F32, name="upd_sb")
-            for t, tokens in pieces:
-                proj_ps = banks.tile([P, BANK], F32, tag="sum")
-                for db in range(D_BLOCKS):
-                    nc.tensor.matmul(
-                        proj_ps[:],
-                        w_sb[cb, db // HALF][:, db % HALF, :],
-                        x_sb[db, t],
-                        start=db == 0,
-                        stop=db == D_BLOCKS - 1,
-                    )
-                copy_out(cb, t)(proj_sb[:, tokens], proj_ps[:])
-            for t, tokens in pieces:
-                upd_ps = banks.tile([P, BANK], F32, tag="sum")
-                nc.tensor.matmul(upd_ps[:], b_sb[:, c_span], h_sb[:, tokens], start=True, stop=True)
-                copy_out(cb, t)(upd_sb[:, tokens], upd_ps[:])
+            copy_last_tokens = nc.vector.tensor_copy if cb == 0 else nc.scalar.copy
+            nc.scalar.copy(proj_sb[:, PROJ_PIECES[0]], project(cb, PROJ_PIECES[0], banks, "sum"))
+            copy_last_tokens(proj_sb[:, PROJ_PIECES[1]], project(cb, PROJ_PIECES[1], late_bank, "late"))
+            nc.scalar.copy(upd_sb[:, TOKEN_PIECES[0]], update(cb, 0))
+            copy_last_tokens(upd_sb[:, TOKEN_PIECES[1]], update(cb, 1))
+            copy_last_tokens(proj_sb[:, PROJ_PIECES[2]], project(cb, PROJ_PIECES[2], banks, "sum"))
 
             nc.vector.tensor_tensor(windows[cb][:].indirect(offsets[:]), proj_sb[:], upd_sb[:], ADD)
             nc.sync.dma_start(out[c_span, :], windows[cb][:])

@@ -12,7 +12,7 @@ LAST = BANK // 4
 PROJ_PIECES = [slice(0, BANK), slice(BANK, N - LAST), slice(N - LAST, N)]
 HALF = D_BLOCKS // 2
 SUM_BANKS, LATE_BANKS = 4, 1
-WARM_UP_MATMULS = 3
+WARM_UP_MATMULS = 4
 
 FLOPS = 2 * N * (D * C + D * K + K * C)
 
@@ -25,11 +25,13 @@ def tile_qkvparallellinearwithlora_b_kernel(tc, base, x, w_q, a_w, b_w, scal, se
         tc.psum_pool(name="banks", bufs=SUM_BANKS) as banks,
         tc.psum_pool(name="late_bank", bufs=LATE_BANKS) as late_bank,
     ):
-        zeros = held.tile([P, BANK], BF16, name="zeros")
-        nc.gpsimd.memset(zeros[:], 0.0)
+        zero = held.tile([P, 2], BF16, name="zero")
+        nc.gpsimd.memset(zero[:], 0.0)
+        zero_weights = zero[:, 0:1].to_broadcast([P, P])
+        zeros = zero[:, 0:1].to_broadcast([P, BANK])
         unread_ps = banks.tile([P, BANK], F32, tag="sum")
         for i in range(WARM_UP_MATMULS):
-            nc.tensor.matmul(unread_ps[:], zeros[:, 0:P], zeros[:], start=True, stop=True)
+            nc.tensor.matmul(unread_ps[:], zero_weights, zeros, start=True, stop=True)
 
         x_blocks = x.rearrange("(p db) n -> p db n", db=D_BLOCKS)
         w_blocks = w_q.rearrange("(p db) c -> p db c", db=D_BLOCKS)
@@ -120,12 +122,12 @@ def tile_qkvparallellinearwithlora_b_kernel(tc, base, x, w_q, a_w, b_w, scal, se
             c_span = slice(cb * P, (cb + 1) * P)
             proj_sb = staged.tile([P, N], F32, name="proj_sb")
             upd_sb = staged.tile([P, N], F32, name="upd_sb")
-            copy_last_tokens = nc.vector.tensor_copy if cb == 0 else nc.scalar.copy
+            copy_late = nc.vector.tensor_copy if cb == 0 else nc.scalar.copy
             nc.scalar.copy(proj_sb[:, PROJ_PIECES[0]], project(cb, PROJ_PIECES[0], banks, "sum"))
-            copy_last_tokens(proj_sb[:, PROJ_PIECES[1]], project(cb, PROJ_PIECES[1], late_bank, "late"))
-            nc.scalar.copy(upd_sb[:, TOKEN_PIECES[0]], update(cb, 0))
-            copy_last_tokens(upd_sb[:, TOKEN_PIECES[1]], update(cb, 1))
-            copy_last_tokens(proj_sb[:, PROJ_PIECES[2]], project(cb, PROJ_PIECES[2], banks, "sum"))
+            copy_late(proj_sb[:, PROJ_PIECES[1]], project(cb, PROJ_PIECES[1], late_bank, "late"))
+            for t, tokens in pieces:
+                nc.scalar.copy(upd_sb[:, tokens], update(cb, t))
+            copy_late(proj_sb[:, PROJ_PIECES[2]], project(cb, PROJ_PIECES[2], banks, "sum"))
 
             nc.vector.tensor_tensor(windows[cb][:].indirect(offsets[:]), proj_sb[:], upd_sb[:], ADD)
             nc.sync.dma_start(out[c_span, :], windows[cb][:])

@@ -75,7 +75,7 @@ def tile_qkvparallellinearwithlora_b_kernel(tc, base, x, w_q, a_w, b_w, scal, se
         scal_sb = held.tile([P, 1], F32, name="scal_sb")
         nc.sync.dma_start(scal_sb[:], scal)
         b_sb = held.tile([P, C], BF16, name="b_sb")
-        nc.sync.dma_start(b_sb[:], b_w)
+        nc.sync.dma_start(b_sb[:, 0:P], b_w[:, 0:P])
 
         offsets = held.tile([P, N // 16], U16, name="offsets")
         nc.sync.dma_start(offsets[:], offs)
@@ -85,6 +85,8 @@ def tile_qkvparallellinearwithlora_b_kernel(tc, base, x, w_q, a_w, b_w, scal, se
             window = held.tile([P, S], F32, name=f"window{cb}")
             nc.sync.dma_start(window[:], base[cb * P : (cb + 1) * P, :])
             windows.append(window)
+            if cb == 0:
+                nc.sync.dma_start(b_sb[:, P:C], b_w[:, P:C])
             if cb + 1 < C_BLOCKS:
                 load_w(cb + 1, 0)
                 load_w(cb + 1, 1)

@@ -67,8 +67,9 @@ def tile_qkvparallellinearwithlora_b_kernel(tc, base, x, w_q, a_w, b_w, scal, se
             load_a(half)
             for db in range(half * HALF, (half + 1) * HALF):
                 load_x(db, split=db == 0)
-                if db == half * HALF:
-                    load_w(0, half)
+                if db == 0:
+                    load_w(0, 0)
+        load_w(0, 1)
 
         sel_sb = held.tile([P, N], F32, name="sel_sb")
         nc.sync.dma_start(sel_sb[:], sel)

import concourse.mybir as mybir

BF16, F32, U16 = mybir.dt.bfloat16, mybir.dt.float32, mybir.dt.uint16
MULT, ADD = mybir.AluOpType.mult, mybir.AluOpType.add

P = 128
C, D, S, N, K = 1024, 1024, 2048, 1024, 128
C_BLOCKS, D_BLOCKS = C // P, D // P
BANK = 512
TOKEN_PIECES = [slice(t, t + BANK) for t in range(0, N, BANK)]
LAST = BANK // 4
PROJ_PIECES = [slice(0, BANK), slice(BANK, N - LAST), slice(N - LAST, N)]
HALF = D_BLOCKS // 2
SUM_BANKS, LATE_BANKS = 4, 1
WARM_UP_MATMULS = 4

FLOPS = 2 * N * (D * C + D * K + K * C)


def tile_qkvparallellinearwithlora_b_kernel(tc, base, x, w_q, a_w, b_w, scal, sel, offs, out):
    nc = tc.nc
    with (
        tc.tile_pool(name="held", bufs=1) as held,
        tc.tile_pool(name="staged", bufs=C_BLOCKS) as staged,
        tc.psum_pool(name="banks", bufs=SUM_BANKS) as banks,
        tc.psum_pool(name="late_bank", bufs=LATE_BANKS) as late_bank,
    ):
        zero = held.tile([P, 2], BF16, name="zero")
        nc.gpsimd.memset(zero[:], 0.0)
        zero_weights = zero[:, 0:1].to_broadcast([P, P])
        zeros = zero[:, 0:1].to_broadcast([P, BANK])
        unread_ps = banks.tile([P, BANK], F32, tag="sum")
        for i in range(WARM_UP_MATMULS):
            nc.tensor.matmul(unread_ps[:], zero_weights, zeros, start=True, stop=True)

        x_blocks = x.rearrange("(p db) n -> p db n", db=D_BLOCKS)
        w_blocks = w_q.rearrange("(p db) c -> p db c", db=D_BLOCKS)
        a_blocks = a_w.rearrange("(p db) k -> p db k", db=D_BLOCKS)
        x_sb = {}
        w_sb = {}
        a_sb = {}
        pieces = list(enumerate(TOKEN_PIECES))

        def load_x(db, split):
            if split:
                for t, tokens in pieces:
                    x_piece = held.tile([P, BANK], BF16, name=f"x{db}_{t}")
                    nc.sync.dma_start(x_piece[:], x_blocks[:, db, tokens])
                    x_sb[db, t] = x_piece[:]
            else:
                x_blk = held.tile([P, N], BF16, name=f"x{db}")
                nc.sync.dma_start(x_blk[:], x_blocks[:, db, :])
                for t, tokens in pieces:
                    x_sb[db, t] = x_blk[:, tokens]

        def load_w(cb, half):
            w_sb[cb, half] = held.tile([P, HALF, P], BF16, name=f"w{cb}_{half}")
            nc.sync.dma_start(
                w_sb[cb, half][:], w_blocks[:, half * HALF : (half + 1) * HALF, cb * P : (cb + 1) * P]
            )

        def load_a(half):
            a_sb[half] = held.tile([P, HALF, K], BF16, name=f"a{half}")
            nc.sync.dma_start(a_sb[half][:], a_blocks[:, half * HALF : (half + 1) * HALF, :])

        for half in range(2):
            load_a(half)
            for db in range(half * HALF, (half + 1) * HALF):
                load_x(db, split=db == 0)
                if db == 0:
                    load_w(0, 0)
        load_w(0, 1)

        sel_sb = held.tile([P, N], F32, name="sel_sb")
        nc.sync.dma_start(sel_sb[:], sel)
        scal_sb = held.tile([P, 1], F32, name="scal_sb")
        nc.sync.dma_start(scal_sb[:], scal)
        b_sb = held.tile([P, C], BF16, name="b_sb")
        nc.sync.dma_start(b_sb[:, 0:P], b_w[:, 0:P])

        offsets = held.tile([P, N // 16], U16, name="offsets")
        nc.sync.dma_start(offsets[:], offs)

        windows = []
        for cb in range(C_BLOCKS):
            window = held.tile([P, S], F32, name=f"window{cb}")
            nc.sync.dma_start(window[:], base[cb * P : (cb + 1) * P, :])
            windows.append(window)
            if cb == 0:
                nc.sync.dma_start(b_sb[:, P:C], b_w[:, P:C])
            if cb + 1 < C_BLOCKS:
                load_w(cb + 1, 0)
                load_w(cb + 1, 1)

        h_sb = held.tile([P, N], BF16, name="h_sb")
        for t, tokens in pieces:
            h_ps = banks.tile([P, BANK], F32, tag="sum")
            for db in range(D_BLOCKS):
                nc.tensor.matmul(
                    h_ps[:], a_sb[db // HALF][:, db % HALF, :], x_sb[db, t], start=db == 0, stop=db == D_BLOCKS - 1
                )
            nc.vector.scalar_tensor_tensor(h_sb[:, tokens], h_ps[:], scal_sb[:, 0:1], sel_sb[:, tokens], MULT, MULT)

        def update(cb, t):
            ps = banks.tile([P, BANK], F32, name="upd_ps", tag="sum")
            nc.tensor.matmul(ps[:], b_sb[:, cb * P : (cb + 1) * P], h_sb[:, TOKEN_PIECES[t]], start=True, stop=True)
            return ps[:]

        def project(cb, tokens, pool, tag):
            ps = pool.tile([P, BANK], F32, name="proj_ps", tag=tag)
            width = tokens.stop - tokens.start
            t = tokens.start // BANK
            columns = slice(tokens.start - t * BANK, tokens.stop - t * BANK)
            for db in range(D_BLOCKS):
                nc.tensor.matmul(
                    ps[:, 0:width],
                    w_sb[cb, db // HALF][:, db % HALF, :],
                    x_sb[db, t][:, columns],
                    start=db == 0,
                    stop=db == D_BLOCKS - 1,
                )
            return ps[:, 0:width]

        for cb in range(C_BLOCKS):
            c_span = slice(cb * P, (cb + 1) * P)
            proj_sb = staged.tile([P, N], F32, name="proj_sb")
            upd_sb = staged.tile([P, N], F32, name="upd_sb")
            copy_late = nc.vector.tensor_copy if cb == 0 else nc.scalar.copy
            nc.scalar.copy(proj_sb[:, PROJ_PIECES[0]], project(cb, PROJ_PIECES[0], banks, "sum"))
            copy_late(proj_sb[:, PROJ_PIECES[1]], project(cb, PROJ_PIECES[1], late_bank, "late"))
            for t, tokens in pieces:
                nc.scalar.copy(upd_sb[:, tokens], update(cb, t))
            copy_late(proj_sb[:, PROJ_PIECES[2]], project(cb, PROJ_PIECES[2], banks, "sum"))

            nc.vector.tensor_tensor(windows[cb][:].indirect(offsets[:]), proj_sb[:], upd_sb[:], ADD)
            nc.sync.dma_start(out[c_span, :], windows[cb][:])
